import numpy as np
import ml_dtypes


def mxq(x, axis, fmt="e4m3"):
    dtype, down = {"e4m3": (ml_dtypes.float8_e4m3fn, 7), "e5m2": (ml_dtypes.float8_e5m2, 14)}[fmt]
    v = np.moveaxis(np.asarray(x, np.float32).astype(ml_dtypes.bfloat16).astype(np.float64), axis, -1)
    blocks = v.reshape(v.shape[:-1] + (-1, 32))
    amax = np.abs(blocks).max(-1, keepdims=True)
    byte = np.maximum(np.where(amax > 0, np.frexp(amax)[1] - 1 + 127, 0) - down, 1)
    scale = np.exp2(byte - 127.0)
    codes = (blocks / scale).astype(np.float32).astype(dtype).astype(np.float64)
    return np.moveaxis((codes * scale).reshape(v.shape), -1, axis)


WIDE = False


def mx_kscale(k):
    if not WIDE:
        return np.ones(k)
    levels = np.array([10, -10, 5, -5, 0])
    a = np.random.permutation(np.resize(levels, k // 512 * 4)).reshape(k // 512, 4)
    idx = np.arange(k)
    return np.exp2(a[idx // 512, idx % 128 // 32])


BF16 = ml_dtypes.bfloat16


def bf(x):
    return np.asarray(x, np.float32).astype(BF16)


def f64(x):
    return np.asarray(x).astype(np.float64)


B, NH, T, D, N, CK = 1, 6, 1024, 512, 256, 512
KD = NH * N
EPS_LN = 1e-5
TARGET_ACTIVITY = 0.1


def layernorm(v):
    m = np.mean(v, axis=-1, keepdims=True)
    var = np.mean((v - m) ** 2, axis=-1, keepdims=True)
    return (v - m) / np.sqrt(var + EPS_LN)


def setup_inputs():
    t = mx_kscale(KD)
    xy = np.maximum(np.random.standard_normal((B, NH, T, N)) * 0.5, 0.0) * np.maximum(np.random.standard_normal((B, NH, T, N)), 0.0)
    return {'xy_sparse': bf(xy * t.reshape(NH, 1, N)),
            'decoder': bf(np.random.standard_normal((KD, D)) * 2.0 / np.sqrt(KD) / t[:, None]),
            'x': bf(np.random.standard_normal((B, 1, T, D))),
            'scale': bf(1.0 + 0.1 * np.random.standard_normal(D)),
            'running_activity': bf(TARGET_ACTIVITY * np.exp(0.5 * np.random.standard_normal(D)))}


def reference(xy_sparse, decoder, x, scale, running_activity):
    flat = f64(xy_sparse).transpose(0, 2, 1, 3).reshape(B, 1, T, KD)
    y_mlp = mxq(flat, 3, 'e4m3') @ mxq(f64(decoder), 0, 'e4m3')
    y = layernorm(y_mlp)
    regulation = TARGET_ACTIVITY / (f64(running_activity) + 1e-6)
    y = y * np.sqrt(regulation) * f64(scale)
    return layernorm(f64(x) + y)

@@ -1,0 +1,246 @@
+from contextlib import ExitStack
+
+import concourse.mybir as mybir
+from concourse.masks import make_identity
+
+F32 = mybir.dt.float32
+BF16 = mybir.dt.bfloat16
+U32 = mybir.dt.uint32
+U8 = mybir.dt.uint8
+FP8X4 = mybir.dt.float8_e4m3fn_x4
+ALU = mybir.AluOpType
+ACT = mybir.ActivationFunctionType
+
+P = 128
+PACK = 4
+K_PASS = P * PACK
+
+HEADS = 6
+TOKENS = 1024
+FEATS = 256
+D = 512
+PASSES = HEADS * FEATS // K_PASS
+HEADS_PER_PASS = K_PASS // FEATS
+WORDS = FEATS // 2
+TILES = TOKENS // P
+PAIR = 2
+PAIRS = TILES // PAIR
+GAIN_ROWS = D // P
+
+EPS_LN = 1e-5
+EPS_ACTIVITY = 1e-6
+TARGET_ACTIVITY = 0.1
+
+FLOPS = 2 * TOKENS * HEADS * FEATS * D
+
+
+def tile_bdhlayer_pc_kernel(tc, xy_sparse, decoder, x, scale, running_activity, out):
+    nc = tc.nc
+
+    xy_view = xy_sparse[0].rearrange("h (p n) f -> p h n f", n=TILES)
+    x_view = x[0, 0].rearrange("(p n) d -> p n d", n=TILES)
+    out_view = out[0, 0].rearrange("(p n) d -> p n d", n=TILES)
+    dec_view = decoder.rearrange("(g u q e) d -> q g u (e d)", g=PASSES, u=HEADS_PER_PASS, e=2)
+
+    with ExitStack() as ctx:
+        const = ctx.enter_context(tc.tile_pool(name="const", bufs=1))
+        loads = ctx.enter_context(tc.tile_pool(name="loads", bufs=PAIRS))
+        front = ctx.enter_context(tc.tile_pool(name="front", bufs=2))
+        work = ctx.enter_context(tc.tile_pool(name="work", bufs=3))
+        small = ctx.enter_context(tc.tile_pool(name="small", bufs=4))
+        psum_t = ctx.enter_context(tc.psum_pool(name="psum_t", bufs=4))
+        psum_y = ctx.enter_context(tc.psum_pool(name="psum_y", bufs=4))
+
+        ident = const.tile([P, P], F32)
+        make_identity(nc, ident[:])
+        eps_ln = const.tile([P, 1], F32)
+        nc.vector.memset(eps_ln[:], EPS_LN)
+        vectors = const.tile([P, 2, P], BF16)
+        nc.vector.memset(vectors[:], 1.0)
+
+        nc.scalar.dma_start(
+            out=vectors[0:GAIN_ROWS, 0, :],
+            in_=running_activity.rearrange("(j c) -> j c", j=GAIN_ROWS),
+        )
+        nc.scalar.dma_start(
+            out=vectors[0:GAIN_ROWS, 1, :], in_=scale.rearrange("(j c) -> j c", j=GAIN_ROWS)
+        )
+
+        xy_tiles = []
+        x_tiles = []
+
+        def load_pair(j):
+            xy_sb = loads.tile([P, HEADS, PAIR, FEATS], BF16, name="xy_sb")
+            nc.sync.dma_start(out=xy_sb[:], in_=xy_view[:, :, PAIR * j : PAIR * (j + 1), :])
+            xy_tiles.append(xy_sb)
+
+        def load_x(j):
+            x_sb = loads.tile([P, PAIR, D], BF16, name="x_sb")
+            nc.sync.dma_start(out=x_sb[:], in_=x_view[:, PAIR * j : PAIR * (j + 1), :])
+            x_tiles.append(x_sb)
+
+        load_pair(0)
+        dec_raw = const.tile([P, PASSES, PACK, D], BF16)
+        for g in range(PASSES):
+            nc.sync.dma_start(
+                out=dec_raw[:, g].rearrange("p (u e) d -> p u (e d)", u=HEADS_PER_PASS),
+                in_=dec_view[:, g],
+            )
+        load_x(0)
+        for j in range(1, PAIRS):
+            load_pair(j)
+            load_x(j)
+
+        shifted = const.tile([P, P], F32)
+        nc.vector.tensor_scalar(
+            out=shifted[:], in0=vectors[:, 0, :], scalar1=EPS_ACTIVITY, scalar2=None, op0=ALU.add
+        )
+        inverse = const.tile([P, P], F32)
+        nc.vector.reciprocal(out=inverse[:], in_=shifted[:])
+        regulation = const.tile([P, P], F32)
+        nc.scalar.activation(out=regulation[:], in_=inverse[:], func=ACT.Sqrt, scale=TARGET_ACTIVITY)
+        gain_rows = const.tile([P, P], F32)
+        nc.vector.tensor_tensor(
+            out=gain_rows[:], in0=regulation[:], in1=vectors[:, 1, :], op=ALU.mult
+        )
+        gain_ps = psum_y.tile([P, D], F32, name="acc")
+        for j in range(GAIN_ROWS):
+            nc.tensor.matmul(
+                out=gain_ps[:, P * j : P * (j + 1)],
+                lhsT=ident[:, j : j + 1].to_broadcast([P, P]),
+                rhs=gain_rows[:],
+                start=True,
+                stop=True,
+            )
+        gain = const.tile([P, D], F32)
+        nc.vector.tensor_copy(out=gain[:], in_=gain_ps[:])
+
+        dec_grouped = const.tile([P, PASSES, D, PACK], BF16, align_bytes=64)
+        dec_codes = const.tile([P, PASSES, D], U32, align_bytes=64)
+        dec_scales = const.tile([P, PASSES, D], U8, align_bytes=64)
+
+        def regroup_decoder(g):
+            nc.vector.tensor_copy(
+                out=dec_grouped[:, g].rearrange("p (c i) t -> p c t i", i=4),
+                in_=dec_raw[:, g].rearrange("p t (c i) -> p c t i", i=4),
+            )
+
+        def quantise_decoder(g):
+            nc.vector.quantize_mx(
+                out=dec_codes[:, g, :].bitcast(FP8X4),
+                scales=dec_scales[:, g, :],
+                in_=dec_grouped[:, g].rearrange("p d t -> p (d t)"),
+            )
+
+        regroup_decoder(0)
+        for g in range(1, PASSES):
+            regroup_decoder(g)
+            quantise_decoder(g - 1)
+        quantise_decoder(PASSES - 1)
+
+        def quantise_pair(j):
+            xy_words = xy_tiles[j][:].bitcast(F32)
+            xy_codes = front.tile([P, PASSES, PAIR * P], U32, align_bytes=64, name="xy_codes")
+            xy_scales = front.tile([P, PASSES, PAIR * P], U8, align_bytes=64, name="xy_scales")
+            banks = []
+            for g in range(PASSES):
+                bank = psum_t.tile([P, PAIR, HEADS_PER_PASS, P], F32, name="bank")
+                for i in range(PAIR):
+                    for u in range(HEADS_PER_PASS):
+                        nc.tensor.transpose(
+                            bank[:, i, u, :], xy_words[:, HEADS_PER_PASS * g + u, i, :], ident[:]
+                        )
+                banks.append(bank)
+            for g in range(PASSES):
+                xy_grouped = front.tile(
+                    [P, PAIR, P, PACK], BF16, align_bytes=64, name="xy_grouped", bufs=2 * PASSES
+                )
+                nc.scalar.copy(
+                    out=xy_grouped[:].bitcast(F32), in_=banks[g][:].rearrange("p i u r -> p i r u")
+                )
+                nc.vector.quantize_mx(
+                    out=xy_codes[:, g, :].bitcast(FP8X4),
+                    scales=xy_scales[:, g, :],
+                    in_=xy_grouped[:].rearrange("p i r t -> p (i r t)"),
+                )
+            return xy_codes, xy_scales
+
+        def finish_tile(xy_codes, xy_scales, i, x_row, out_row):
+            tokens = slice(P * i, P * (i + 1))
+            acc = psum_y.tile([P, D], F32, name="acc")
+            for g in range(PASSES):
+                nc.tensor.matmul_mx(
+                    out=acc[:],
+                    lhsT=xy_codes[:, g, tokens].bitcast(FP8X4),
+                    lhsT_scale=xy_scales[:, g, tokens],
+                    rhs=dec_codes[:, g, :].bitcast(FP8X4),
+                    rhs_scale=dec_scales[:, g, :],
+                    start=(g == 0),
+                    stop=(g == PASSES - 1),
+                )
+            stats = small.tile([P, 6], F32, name="stats")
+            nc.vector.bn_stats(out=stats[:], in_=acc[:])
+            mean_var = small.tile([P, 2], F32, name="mean_var")
+            nc.vector.bn_aggr(out=mean_var[:], in_=stats[:])
+            std1 = small.tile([P, 1], F32, name="std1")
+            nc.scalar.activation(out=std1[:], in_=mean_var[:, 1:2], func=ACT.Sqrt, bias=eps_ln[:])
+            centred = work.tile([P, D], F32, name="centred")
+            nc.vector.scalar_tensor_tensor(
+                out=centred[:],
+                in0=acc[:],
+                scalar=mean_var[:, 0:1],
+                in1=gain[:],
+                op0=ALU.subtract,
+                op1=ALU.mult,
+            )
+            rstd1 = small.tile([P, 1], F32, name="rstd1")
+            nc.vector.reciprocal(out=rstd1[:], in_=std1[:])
+            z = work.tile([P, D], F32, name="z")
+            z_sum = small.tile([P, 1], F32, name="z_sum")
+            nc.vector.scalar_tensor_tensor(
+                out=z[:],
+                in0=centred[:],
+                scalar=rstd1[:],
+                in1=x_row,
+                op0=ALU.mult,
+                op1=ALU.add,
+                accum_out=z_sum[:],
+            )
+            squares = work.tile([P, D], F32, name="squares")
+            sum_sq = small.tile([P, 1], F32, name="sum_sq")
+            nc.scalar.activation(
+                out=squares[:],
+                in_=z[:],
+                func=ACT.Square,
+                scale=-float(D),
+                bias=z_sum[:],
+                accum_out=sum_sq[:],
+            )
+            std2 = small.tile([P, 1], F32, name="std2")
+            nc.scalar.activation(
+                out=std2[:], in_=sum_sq[:], func=ACT.Sqrt, scale=1.0 / float(D * D * D), bias=eps_ln[:]
+            )
+            rstd2 = small.tile([P, 1], F32, name="rstd2")
+            nc.vector.reciprocal(out=rstd2[:], in_=std2[:])
+            shift2 = small.tile([P, 1], F32, name="shift2")
+            nc.vector.tensor_scalar(
+                out=shift2[:],
+                in0=z_sum[:],
+                scalar1=rstd2[:],
+                scalar2=-1.0 / float(D),
+                op0=ALU.mult,
+                op1=ALU.mult,
+            )
+            nc.scalar.activation(
+                out=out_row, in_=z[:], func=ACT.Identity, scale=rstd2[:], bias=shift2[:]
+            )
+
+        quantised = [quantise_pair(0)]
+        for j in range(PAIRS):
+            if j + 1 < PAIRS:
+                quantised.append(quantise_pair(j + 1))
+            xy_codes, xy_scales = quantised[j]
+            result = work.tile([P, PAIR, D], F32, name="result")
+            for i in range(PAIR):
+                finish_tile(xy_codes, xy_scales, i, x_tiles[j][:, i, :], result[:, i, :])
+            nc.sync.dma_start(out=out_view[:, PAIR * j : PAIR * (j + 1), :], in_=result[:])

@@ -26,6 +26,8 @@ TILES = TOKENS // P
 PAIR = 2
 PAIRS = TILES // PAIR
 GAIN_ROWS = D // P
+RUN = 4
+DEC_COLS_VECTOR = (2 * D // 3) // RUN * RUN
 
 EPS_LN = 1e-5
 EPS_ACTIVITY = 1e-6
@@ -45,31 +47,44 @@ def tile_bdhlayer_pc_kernel(tc, xy_sparse, decoder, x, scale, running_activity, 
     with ExitStack() as ctx:
         const = ctx.enter_context(tc.tile_pool(name="const", bufs=1))
         loads = ctx.enter_context(tc.tile_pool(name="loads", bufs=PAIRS))
-        front = ctx.enter_context(tc.tile_pool(name="front", bufs=2))
         work = ctx.enter_context(tc.tile_pool(name="work", bufs=3))
         small = ctx.enter_context(tc.tile_pool(name="small", bufs=4))
-        psum_t = ctx.enter_context(tc.psum_pool(name="psum_t", bufs=4))
-        psum_y = ctx.enter_context(tc.psum_pool(name="psum_y", bufs=4))
+        psum_t = ctx.enter_context(tc.psum_pool(name="psum_t", bufs=2 * PASSES))
+        psum_y = ctx.enter_context(tc.psum_pool(name="psum_y", bufs=2))
+        ctx.enter_context(tc.manual_schedule())
 
         ident = const.tile([P, P], F32)
         make_identity(nc, ident[:])
         eps_ln = const.tile([P, 1], F32)
         nc.vector.memset(eps_ln[:], EPS_LN)
+        eps_activity = const.tile([P, 1], F32)
+        nc.vector.memset(eps_activity[:], EPS_ACTIVITY / TARGET_ACTIVITY)
         vectors = const.tile([P, 2, P], BF16)
         nc.vector.memset(vectors[:], 1.0)
 
-        nc.scalar.dma_start(
+        dec_raw = const.tile([P, PASSES, PACK, D], BF16)
+
+        def load_decoder(g):
+            nc.sync.dma_start(
+                out=dec_raw[:, g].rearrange("p (u e) d -> p u (e d)", u=HEADS_PER_PASS),
+                in_=dec_view[:, g],
+            )
+
+        load_decoder(0)
+        nc.sync.dma_start(
             out=vectors[0:GAIN_ROWS, 0, :],
             in_=running_activity.rearrange("(j c) -> j c", j=GAIN_ROWS),
         )
-        nc.scalar.dma_start(
+        nc.sync.dma_start(
             out=vectors[0:GAIN_ROWS, 1, :], in_=scale.rearrange("(j c) -> j c", j=GAIN_ROWS)
         )
+        for g in range(1, PASSES):
+            load_decoder(g)
 
         xy_tiles = []
         x_tiles = []
 
-        def load_pair(j):
+        def load_xy(j):
             xy_sb = loads.tile([P, HEADS, PAIR, FEATS], BF16, name="xy_sb")
             nc.sync.dma_start(out=xy_sb[:], in_=xy_view[:, :, PAIR * j : PAIR * (j + 1), :])
             xy_tiles.append(xy_sb)
@@ -79,26 +94,20 @@ def tile_bdhlayer_pc_kernel(tc, xy_sparse, decoder, x, scale, running_activity, 
             nc.sync.dma_start(out=x_sb[:], in_=x_view[:, PAIR * j : PAIR * (j + 1), :])
             x_tiles.append(x_sb)
 
-        load_pair(0)
-        dec_raw = const.tile([P, PASSES, PACK, D], BF16)
-        for g in range(PASSES):
-            nc.sync.dma_start(
-                out=dec_raw[:, g].rearrange("p (u e) d -> p u (e d)", u=HEADS_PER_PASS),
-                in_=dec_view[:, g],
-            )
-        load_x(0)
-        for j in range(1, PAIRS):
-            load_pair(j)
+        load_xy(0)
+        for j in range(PAIRS):
+            if j + 1 < PAIRS:
+                load_xy(j + 1)
             load_x(j)
 
-        shifted = const.tile([P, P], F32)
-        nc.vector.tensor_scalar(
-            out=shifted[:], in0=vectors[:, 0, :], scalar1=EPS_ACTIVITY, scalar2=None, op0=ALU.add
-        )
-        inverse = const.tile([P, P], F32)
-        nc.vector.reciprocal(out=inverse[:], in_=shifted[:])
         regulation = const.tile([P, P], F32)
-        nc.scalar.activation(out=regulation[:], in_=inverse[:], func=ACT.Sqrt, scale=TARGET_ACTIVITY)
+        nc.scalar.activation(
+            out=regulation[:],
+            in_=vectors[:, 0, :],
+            func=ACT.Abs_reciprocal_sqrt,
+            scale=1.0 / TARGET_ACTIVITY,
+            bias=eps_activity[:],
+        )
         gain_rows = const.tile([P, P], F32)
         nc.vector.tensor_tensor(
             out=gain_rows[:], in0=regulation[:], in1=vectors[:, 1, :], op=ALU.mult
@@ -113,7 +122,6 @@ def tile_bdhlayer_pc_kernel(tc, xy_sparse, decoder, x, scale, running_activity, 
                 stop=True,
             )
         gain = const.tile([P, D], F32)
-        nc.vector.tensor_copy(out=gain[:], in_=gain_ps[:])
 
         dec_grouped = const.tile([P, PASSES, D, PACK], BF16, align_bytes=64)
         dec_codes = const.tile([P, PASSES, D], U32, align_bytes=64)
@@ -121,8 +129,12 @@ def tile_bdhlayer_pc_kernel(tc, xy_sparse, decoder, x, scale, running_activity, 
 
         def regroup_decoder(g):
             nc.vector.tensor_copy(
-                out=dec_grouped[:, g].rearrange("p (c i) t -> p c t i", i=4),
-                in_=dec_raw[:, g].rearrange("p t (c i) -> p c t i", i=4),
+                out=dec_grouped[:, g, :DEC_COLS_VECTOR, :].rearrange("p (c i) t -> p c t i", i=RUN),
+                in_=dec_raw[:, g, :, :DEC_COLS_VECTOR].rearrange("p t (c i) -> p c t i", i=RUN),
+            )
+            nc.scalar.copy(
+                out=dec_grouped[:, g, DEC_COLS_VECTOR:, :].rearrange("p (c i) t -> p c t i", i=RUN),
+                in_=dec_raw[:, g, :, DEC_COLS_VECTOR:].rearrange("p t (c i) -> p c t i", i=RUN),
             )
 
         def quantise_decoder(g):
@@ -133,114 +145,173 @@ def tile_bdhlayer_pc_kernel(tc, xy_sparse, decoder, x, scale, running_activity, 
             )
 
         regroup_decoder(0)
+        nc.scalar.copy(out=gain[:], in_=gain_ps[:])
         for g in range(1, PASSES):
             regroup_decoder(g)
             quantise_decoder(g - 1)
         quantise_decoder(PASSES - 1)
 
-        def quantise_pair(j):
+        banks = {}
+        grouped = {}
+        codes = {}
+        acc = {}
+        stat = {}
+        centred = {}
+        z = {}
+
+        def transpose_pair(j):
             xy_words = xy_tiles[j][:].bitcast(F32)
-            xy_codes = front.tile([P, PASSES, PAIR * P], U32, align_bytes=64, name="xy_codes")
-            xy_scales = front.tile([P, PASSES, PAIR * P], U8, align_bytes=64, name="xy_scales")
-            banks = []
-            for g in range(PASSES):
-                bank = psum_t.tile([P, PAIR, HEADS_PER_PASS, P], F32, name="bank")
-                for i in range(PAIR):
+            banks[j] = [
+                psum_t.tile([P, PAIR, HEADS_PER_PASS, P], F32, name="bank") for g in range(PASSES)
+            ]
+            for i in range(PAIR):
+                for g in range(PASSES):
                     for u in range(HEADS_PER_PASS):
                         nc.tensor.transpose(
-                            bank[:, i, u, :], xy_words[:, HEADS_PER_PASS * g + u, i, :], ident[:]
+                            banks[j][g][:, i, u, :],
+                            xy_words[:, HEADS_PER_PASS * g + u, i, :],
+                            ident[:],
                         )
-                banks.append(bank)
+
+        def evacuate_tile(t):
+            grouped[t] = work.tile([P, PASSES, P, PACK], BF16, align_bytes=64, name="xy_grouped")
             for g in range(PASSES):
-                xy_grouped = front.tile(
-                    [P, PAIR, P, PACK], BF16, align_bytes=64, name="xy_grouped", bufs=2 * PASSES
-                )
                 nc.scalar.copy(
-                    out=xy_grouped[:].bitcast(F32), in_=banks[g][:].rearrange("p i u r -> p i r u")
+                    out=grouped[t][:, g].bitcast(F32),
+                    in_=banks[t // PAIR][g][:, t % PAIR].rearrange("p u r -> p r u"),
                 )
+
+        def quantise_tile(t):
+            xy_codes = work.tile([P, PASSES, P], U32, align_bytes=64, name="xy_codes")
+            xy_scales = work.tile([P, PASSES, P], U8, align_bytes=64, name="xy_scales")
+            for g in range(PASSES):
                 nc.vector.quantize_mx(
                     out=xy_codes[:, g, :].bitcast(FP8X4),
                     scales=xy_scales[:, g, :],
-                    in_=xy_grouped[:].rearrange("p i r t -> p (i r t)"),
+                    in_=grouped[t][:, g].rearrange("p r t -> p (r t)"),
                 )
-            return xy_codes, xy_scales
+            codes[t] = (xy_codes, xy_scales)
 
-        def finish_tile(xy_codes, xy_scales, i, x_row, out_row):
-            tokens = slice(P * i, P * (i + 1))
-            acc = psum_y.tile([P, D], F32, name="acc")
+        def multiply(t):
+            xy_codes, xy_scales = codes[t]
+            acc[t] = psum_y.tile([P, D], F32, name="acc")
             for g in range(PASSES):
                 nc.tensor.matmul_mx(
-                    out=acc[:],
-                    lhsT=xy_codes[:, g, tokens].bitcast(FP8X4),
-                    lhsT_scale=xy_scales[:, g, tokens],
+                    out=acc[t][:],
+                    lhsT=xy_codes[:, g, :].bitcast(FP8X4),
+                    lhsT_scale=xy_scales[:, g, :],
                     rhs=dec_codes[:, g, :].bitcast(FP8X4),
                     rhs_scale=dec_scales[:, g, :],
                     start=(g == 0),
                     stop=(g == PASSES - 1),
                 )
-            stats = small.tile([P, 6], F32, name="stats")
-            nc.vector.bn_stats(out=stats[:], in_=acc[:])
-            mean_var = small.tile([P, 2], F32, name="mean_var")
-            nc.vector.bn_aggr(out=mean_var[:], in_=stats[:])
-            std1 = small.tile([P, 1], F32, name="std1")
-            nc.scalar.activation(out=std1[:], in_=mean_var[:, 1:2], func=ACT.Sqrt, bias=eps_ln[:])
-            centred = work.tile([P, D], F32, name="centred")
+
+        def new_stat(name, t, width):
+            stat[(name, t)] = small.tile([P, width], F32, name=name)
+            return stat[(name, t)]
+
+        def first_stats(t):
+            nc.vector.bn_stats(out=new_stat("partial", t, 6)[:], in_=acc[t][:])
+
+        def first_mean_var(t):
+            nc.vector.bn_aggr(out=new_stat("mean_var", t, 2)[:], in_=stat[("partial", t)][:])
+
+        def first_rstd(t):
+            nc.scalar.activation(
+                out=new_stat("rstd1", t, 1)[:],
+                in_=stat[("mean_var", t)][:, 1:2],
+                func=ACT.Abs_reciprocal_sqrt,
+                bias=eps_ln[:],
+            )
+
+        def centre_and_gain(t):
+            centred[t] = work.tile([P, D], F32, name="centred")
             nc.vector.scalar_tensor_tensor(
-                out=centred[:],
-                in0=acc[:],
-                scalar=mean_var[:, 0:1],
+                out=centred[t][:],
+                in0=acc[t][:],
+                scalar=stat[("mean_var", t)][:, 0:1],
                 in1=gain[:],
                 op0=ALU.subtract,
                 op1=ALU.mult,
             )
-            rstd1 = small.tile([P, 1], F32, name="rstd1")
-            nc.vector.reciprocal(out=rstd1[:], in_=std1[:])
-            z = work.tile([P, D], F32, name="z")
-            z_sum = small.tile([P, 1], F32, name="z_sum")
+
+        def add_residual(t):
+            z[t] = work.tile([P, D], F32, name="z")
             nc.vector.scalar_tensor_tensor(
-                out=z[:],
-                in0=centred[:],
-                scalar=rstd1[:],
-                in1=x_row,
+                out=z[t][:],
+                in0=centred[t][:],
+                scalar=stat[("rstd1", t)][:],
+                in1=x_tiles[t // PAIR][:, t % PAIR, :],
                 op0=ALU.mult,
                 op1=ALU.add,
-                accum_out=z_sum[:],
+                accum_out=new_stat("z_sum", t, 1)[:],
             )
+
+        def second_sum_of_squares(t):
             squares = work.tile([P, D], F32, name="squares")
-            sum_sq = small.tile([P, 1], F32, name="sum_sq")
             nc.scalar.activation(
                 out=squares[:],
-                in_=z[:],
+                in_=z[t][:],
                 func=ACT.Square,
                 scale=-float(D),
-                bias=z_sum[:],
-                accum_out=sum_sq[:],
+                bias=stat[("z_sum", t)][:],
+                accum_out=new_stat("sum_sq", t, 1)[:],
             )
-            std2 = small.tile([P, 1], F32, name="std2")
+
+        def second_rstd(t):
             nc.scalar.activation(
-                out=std2[:], in_=sum_sq[:], func=ACT.Sqrt, scale=1.0 / float(D * D * D), bias=eps_ln[:]
+                out=new_stat("rstd2", t, 1)[:],
+                in_=stat[("sum_sq", t)][:],
+                func=ACT.Abs_reciprocal_sqrt,
+                scale=1.0 / float(D * D * D),
+                bias=eps_ln[:],
             )
-            rstd2 = small.tile([P, 1], F32, name="rstd2")
-            nc.vector.reciprocal(out=rstd2[:], in_=std2[:])
-            shift2 = small.tile([P, 1], F32, name="shift2")
-            nc.vector.tensor_scalar(
-                out=shift2[:],
-                in0=z_sum[:],
-                scalar1=rstd2[:],
+
+        def second_shift(t):
+            nc.gpsimd.tensor_scalar(
+                out=new_stat("shift2", t, 1)[:],
+                in0=stat[("z_sum", t)][:],
+                scalar1=stat[("rstd2", t)][:],
                 scalar2=-1.0 / float(D),
                 op0=ALU.mult,
                 op1=ALU.mult,
             )
-            nc.scalar.activation(
-                out=out_row, in_=z[:], func=ACT.Identity, scale=rstd2[:], bias=shift2[:]
-            )
 
-        quantised = [quantise_pair(0)]
-        for j in range(PAIRS):
-            if j + 1 < PAIRS:
-                quantised.append(quantise_pair(j + 1))
-            xy_codes, xy_scales = quantised[j]
-            result = work.tile([P, PAIR, D], F32, name="result")
-            for i in range(PAIR):
-                finish_tile(xy_codes, xy_scales, i, x_tiles[j][:, i, :], result[:, i, :])
-            nc.sync.dma_start(out=out_view[:, PAIR * j : PAIR * (j + 1), :], in_=result[:])
+        def normalise_and_store(t):
+            result = work.tile([P, D], F32, name="result")
+            nc.scalar.activation(
+                out=result[:],
+                in_=z[t][:],
+                func=ACT.Identity,
+                scale=stat[("rstd2", t)][:],
+                bias=stat[("shift2", t)][:],
+            )
+            nc.sync.dma_start(out=out_view[:, t, :], in_=result[:])
+
+        def live(t):
+            return 0 <= t < TILES
+
+        for t in range(-3, TILES + 2):
+            if live(t):
+                first_stats(t)
+            if live(t + 1):
+                quantise_tile(t + 1)
+                multiply(t + 1)
+            if live(t + 3) and (t + 3) % PAIR == 0:
+                transpose_pair((t + 3) // PAIR)
+            if live(t):
+                first_mean_var(t)
+            if live(t - 2):
+                second_rstd(t - 2)
+                second_shift(t - 2)
+            if live(t + 2):
+                evacuate_tile(t + 2)
+            if live(t):
+                first_rstd(t)
+            if live(t - 2):
+                normalise_and_store(t - 2)
+            if live(t - 1):
+                add_residual(t - 1)
+                second_sum_of_squares(t - 1)
+            if live(t):
+                centre_and_gain(t)

@@ -25,6 +25,7 @@ WORDS = FEATS // 2
 TILES = TOKENS // P
 PAIR = 2
 PAIRS = TILES // PAIR
+PASS_GROUPS = ((0, 2), (2, 3))
 GAIN_ROWS = D // P
 RUN = 4
 DEC_COLS_VECTOR = (2 * D // 3) // RUN * RUN
@@ -49,8 +50,8 @@ def tile_bdhlayer_pc_kernel(tc, xy_sparse, decoder, x, scale, running_activity, 
         loads = ctx.enter_context(tc.tile_pool(name="loads", bufs=PAIRS))
         work = ctx.enter_context(tc.tile_pool(name="work", bufs=3))
         small = ctx.enter_context(tc.tile_pool(name="small", bufs=4))
-        psum_t = ctx.enter_context(tc.psum_pool(name="psum_t", bufs=2 * PASSES))
-        psum_y = ctx.enter_context(tc.psum_pool(name="psum_y", bufs=2))
+        psum_t = ctx.enter_context(tc.psum_pool(name="psum_t", bufs=2))
+        psum_y = ctx.enter_context(tc.psum_pool(name="psum_y", bufs=4))
         ctx.enter_context(tc.manual_schedule())
 
         ident = const.tile([P, P], F32)
@@ -159,36 +160,38 @@ def tile_bdhlayer_pc_kernel(tc, xy_sparse, decoder, x, scale, running_activity, 
         centred = {}
         z = {}
 
-        def transpose_pair(j):
-            xy_words = xy_tiles[j][:].bitcast(F32)
-            banks[j] = [
-                psum_t.tile([P, PAIR, HEADS_PER_PASS, P], F32, name="bank") for g in range(PASSES)
-            ]
-            for i in range(PAIR):
-                for g in range(PASSES):
+        def transpose_tile(t):
+            xy_words = xy_tiles[t // PAIR][:].bitcast(F32)
+            banks[t] = []
+            for first, end in PASS_GROUPS:
+                bank = psum_t.tile(
+                    [P, end - first, HEADS_PER_PASS, P], F32, name="bank%d" % first
+                )
+                for g in range(first, end):
                     for u in range(HEADS_PER_PASS):
                         nc.tensor.transpose(
-                            banks[j][g][:, i, u, :],
-                            xy_words[:, HEADS_PER_PASS * g + u, i, :],
+                            bank[:, g - first, u, :],
+                            xy_words[:, HEADS_PER_PASS * g + u, t % PAIR, :],
                             ident[:],
                         )
+                banks[t].append(bank)
 
         def evacuate_tile(t):
             grouped[t] = work.tile([P, PASSES, P, PACK], BF16, align_bytes=64, name="xy_grouped")
-            for g in range(PASSES):
+            for (first, end), bank in zip(PASS_GROUPS, banks[t]):
                 nc.scalar.copy(
-                    out=grouped[t][:, g].bitcast(F32),
-                    in_=banks[t // PAIR][g][:, t % PAIR].rearrange("p u r -> p r u"),
+                    out=grouped[t][:, first:end].bitcast(F32),
+                    in_=bank[:].rearrange("p g u r -> p g r u"),
                 )
 
         def quantise_tile(t):
             xy_codes = work.tile([P, PASSES, P], U32, align_bytes=64, name="xy_codes")
             xy_scales = work.tile([P, PASSES, P], U8, align_bytes=64, name="xy_scales")
-            for g in range(PASSES):
+            for first, end in PASS_GROUPS:
                 nc.vector.quantize_mx(
-                    out=xy_codes[:, g, :].bitcast(FP8X4),
-                    scales=xy_scales[:, g, :],
-                    in_=grouped[t][:, g].rearrange("p r t -> p (r t)"),
+                    out=xy_codes[:, first:end, :].rearrange("p g r -> p (g r)").bitcast(FP8X4),
+                    scales=xy_scales[:, first:end, :].rearrange("p g r -> p (g r)"),
+                    in_=grouped[t][:, first:end].rearrange("p g r t -> p (g r t)"),
                 )
             codes[t] = (xy_codes, xy_scales)
 
@@ -246,6 +249,14 @@ def tile_bdhlayer_pc_kernel(tc, xy_sparse, decoder, x, scale, running_activity, 
                 op1=ALU.add,
                 accum_out=new_stat("z_sum", t, 1)[:],
             )
+            nc.gpsimd.tensor_scalar(
+                out=new_stat("neg_mean", t, 1)[:],
+                in0=stat[("z_sum", t)][:],
+                scalar1=-1.0 / float(D),
+                scalar2=0.0,
+                op0=ALU.mult,
+                op1=ALU.add,
+            )
 
         def second_sum_of_squares(t):
             squares = work.tile([P, D], F32, name="squares")
@@ -268,16 +279,14 @@ def tile_bdhlayer_pc_kernel(tc, xy_sparse, decoder, x, scale, running_activity, 
             )
 
         def second_shift(t):
-            nc.gpsimd.tensor_scalar(
+            nc.scalar.activation(
                 out=new_stat("shift2", t, 1)[:],
-                in0=stat[("z_sum", t)][:],
-                scalar1=stat[("rstd2", t)][:],
-                scalar2=-1.0 / float(D),
-                op0=ALU.mult,
-                op1=ALU.mult,
+                in_=stat[("neg_mean", t)][:],
+                func=ACT.Identity,
+                scale=stat[("rstd2", t)][:],
             )
 
-        def normalise_and_store(t):
+        def normalise_on_scalar(t):
             result = work.tile([P, D], F32, name="result")
             nc.scalar.activation(
                 out=result[:],
@@ -288,28 +297,44 @@ def tile_bdhlayer_pc_kernel(tc, xy_sparse, decoder, x, scale, running_activity, 
             )
             nc.sync.dma_start(out=out_view[:, t, :], in_=result[:])
 
+        def normalise_on_vector(t):
+            result = work.tile([P, D], F32, name="result")
+            nc.vector.tensor_scalar(
+                out=result[:],
+                in0=z[t][:],
+                scalar1=stat[("neg_mean", t)][:],
+                scalar2=stat[("rstd2", t)][:],
+                op0=ALU.add,
+                op1=ALU.mult,
+            )
+            nc.sync.dma_start(out=out_view[:, t, :], in_=result[:])
+
         def live(t):
             return 0 <= t < TILES
 
-        for t in range(-3, TILES + 2):
+        LAST = TILES - 1
+        for t in range(-4, TILES + 2):
             if live(t):
                 first_stats(t)
-            if live(t + 1):
-                quantise_tile(t + 1)
-                multiply(t + 1)
-            if live(t + 3) and (t + 3) % PAIR == 0:
-                transpose_pair((t + 3) // PAIR)
+            if live(t + 2):
+                quantise_tile(t + 2)
+                multiply(t + 2)
+            if live(t + 4):
+                transpose_tile(t + 4)
             if live(t):
                 first_mean_var(t)
             if live(t - 2):
                 second_rstd(t - 2)
+            if live(t + 3):
+                evacuate_tile(t + 3)
+            if live(t - 2) and t - 2 != LAST:
                 second_shift(t - 2)
-            if live(t + 2):
-                evacuate_tile(t + 2)
             if live(t):
                 first_rstd(t)
-            if live(t - 2):
-                normalise_and_store(t - 2)
+            if live(t - 2) and t - 2 != LAST:
+                normalise_on_scalar(t - 2)
+            if t - 2 == LAST:
+                normalise_on_vector(LAST)
             if live(t - 1):
                 add_residual(t - 1)
                 second_sum_of_squares(t - 1)

from contextlib import ExitStack

import concourse.mybir as mybir
from concourse.masks import make_identity

F32 = mybir.dt.float32
BF16 = mybir.dt.bfloat16
U32 = mybir.dt.uint32
U8 = mybir.dt.uint8
FP8X4 = mybir.dt.float8_e4m3fn_x4
ALU = mybir.AluOpType
ACT = mybir.ActivationFunctionType

P = 128
PACK = 4
K_PASS = P * PACK

HEADS = 6
TOKENS = 1024
FEATS = 256
D = 512
PASSES = HEADS * FEATS // K_PASS
HEADS_PER_PASS = K_PASS // FEATS
WORDS = FEATS // 2
TILES = TOKENS // P
PAIR = 2
PAIRS = TILES // PAIR
PASS_GROUPS = ((0, 2), (2, 3))
GAIN_ROWS = D // P
RUN = 4
DEC_COLS_VECTOR = (2 * D // 3) // RUN * RUN

EPS_LN = 1e-5
EPS_ACTIVITY = 1e-6
TARGET_ACTIVITY = 0.1

FLOPS = 2 * TOKENS * HEADS * FEATS * D


def tile_bdhlayer_pc_kernel(tc, xy_sparse, decoder, x, scale, running_activity, out):
    nc = tc.nc

    xy_view = xy_sparse[0].rearrange("h (p n) f -> p h n f", n=TILES)
    x_view = x[0, 0].rearrange("(p n) d -> p n d", n=TILES)
    out_view = out[0, 0].rearrange("(p n) d -> p n d", n=TILES)
    dec_view = decoder.rearrange("(g u q e) d -> q g u (e d)", g=PASSES, u=HEADS_PER_PASS, e=2)

    with ExitStack() as ctx:
        const = ctx.enter_context(tc.tile_pool(name="const", bufs=1))
        loads = ctx.enter_context(tc.tile_pool(name="loads", bufs=PAIRS))
        work = ctx.enter_context(tc.tile_pool(name="work", bufs=3))
        small = ctx.enter_context(tc.tile_pool(name="small", bufs=4))
        psum_t = ctx.enter_context(tc.psum_pool(name="psum_t", bufs=2))
        psum_y = ctx.enter_context(tc.psum_pool(name="psum_y", bufs=4))
        ctx.enter_context(tc.manual_schedule())

        ident = const.tile([P, P], F32)
        make_identity(nc, ident[:])
        eps_ln = const.tile([P, 1], F32)
        nc.vector.memset(eps_ln[:], EPS_LN)
        eps_activity = const.tile([P, 1], F32)
        nc.vector.memset(eps_activity[:], EPS_ACTIVITY / TARGET_ACTIVITY)
        vectors = const.tile([P, 2, P], BF16)
        nc.vector.memset(vectors[:], 1.0)

        dec_raw = const.tile([P, PASSES, PACK, D], BF16)

        def load_decoder(g):
            nc.sync.dma_start(
                out=dec_raw[:, g].rearrange("p (u e) d -> p u (e d)", u=HEADS_PER_PASS),
                in_=dec_view[:, g],
            )

        load_decoder(0)
        nc.sync.dma_start(
            out=vectors[0:GAIN_ROWS, 0, :],
            in_=running_activity.rearrange("(j c) -> j c", j=GAIN_ROWS),
        )
        nc.sync.dma_start(
            out=vectors[0:GAIN_ROWS, 1, :], in_=scale.rearrange("(j c) -> j c", j=GAIN_ROWS)
        )
        for g in range(1, PASSES):
            load_decoder(g)

        xy_tiles = []
        x_tiles = []

        def load_xy(j):
            xy_sb = loads.tile([P, HEADS, PAIR, FEATS], BF16, name="xy_sb")
            nc.sync.dma_start(out=xy_sb[:], in_=xy_view[:, :, PAIR * j : PAIR * (j + 1), :])
            xy_tiles.append(xy_sb)

        def load_x(j):
            x_sb = loads.tile([P, PAIR, D], BF16, name="x_sb")
            nc.sync.dma_start(out=x_sb[:], in_=x_view[:, PAIR * j : PAIR * (j + 1), :])
            x_tiles.append(x_sb)

        load_xy(0)
        for j in range(PAIRS):
            if j + 1 < PAIRS:
                load_xy(j + 1)
            load_x(j)

        regulation = const.tile([P, P], F32)
        nc.scalar.activation(
            out=regulation[:],
            in_=vectors[:, 0, :],
            func=ACT.Abs_reciprocal_sqrt,
            scale=1.0 / TARGET_ACTIVITY,
            bias=eps_activity[:],
        )
        gain_rows = const.tile([P, P], F32)
        nc.vector.tensor_tensor(
            out=gain_rows[:], in0=regulation[:], in1=vectors[:, 1, :], op=ALU.mult
        )
        gain_ps = psum_y.tile([P, D], F32, name="acc")
        for j in range(GAIN_ROWS):
            nc.tensor.matmul(
                out=gain_ps[:, P * j : P * (j + 1)],
                lhsT=ident[:, j : j + 1].to_broadcast([P, P]),
                rhs=gain_rows[:],
                start=True,
                stop=True,
            )
        gain = const.tile([P, D], F32)

        dec_grouped = const.tile([P, PASSES, D, PACK], BF16, align_bytes=64)
        dec_codes = const.tile([P, PASSES, D], U32, align_bytes=64)
        dec_scales = const.tile([P, PASSES, D], U8, align_bytes=64)

        def regroup_decoder(g):
            nc.vector.tensor_copy(
                out=dec_grouped[:, g, :DEC_COLS_VECTOR, :].rearrange("p (c i) t -> p c t i", i=RUN),
                in_=dec_raw[:, g, :, :DEC_COLS_VECTOR].rearrange("p t (c i) -> p c t i", i=RUN),
            )
            nc.scalar.copy(
                out=dec_grouped[:, g, DEC_COLS_VECTOR:, :].rearrange("p (c i) t -> p c t i", i=RUN),
                in_=dec_raw[:, g, :, DEC_COLS_VECTOR:].rearrange("p t (c i) -> p c t i", i=RUN),
            )

        def quantise_decoder(g):
            nc.vector.quantize_mx(
                out=dec_codes[:, g, :].bitcast(FP8X4),
                scales=dec_scales[:, g, :],
                in_=dec_grouped[:, g].rearrange("p d t -> p (d t)"),
            )

        regroup_decoder(0)
        nc.scalar.copy(out=gain[:], in_=gain_ps[:])
        for g in range(1, PASSES):
            regroup_decoder(g)
            quantise_decoder(g - 1)
        quantise_decoder(PASSES - 1)

        banks = {}
        grouped = {}
        codes = {}
        acc = {}
        stat = {}
        centred = {}
        z = {}

        def transpose_tile(t):
            xy_words = xy_tiles[t // PAIR][:].bitcast(F32)
            banks[t] = []
            for first, end in PASS_GROUPS:
                bank = psum_t.tile(
                    [P, end - first, HEADS_PER_PASS, P], F32, name="bank%d" % first
                )
                for g in range(first, end):
                    for u in range(HEADS_PER_PASS):
                        nc.tensor.transpose(
                            bank[:, g - first, u, :],
                            xy_words[:, HEADS_PER_PASS * g + u, t % PAIR, :],
                            ident[:],
                        )
                banks[t].append(bank)

        def evacuate_tile(t):
            grouped[t] = work.tile([P, PASSES, P, PACK], BF16, align_bytes=64, name="xy_grouped")
            for (first, end), bank in zip(PASS_GROUPS, banks[t]):
                nc.scalar.copy(
                    out=grouped[t][:, first:end].bitcast(F32),
                    in_=bank[:].rearrange("p g u r -> p g r u"),
                )

        def quantise_tile(t):
            xy_codes = work.tile([P, PASSES, P], U32, align_bytes=64, name="xy_codes")
            xy_scales = work.tile([P, PASSES, P], U8, align_bytes=64, name="xy_scales")
            for first, end in PASS_GROUPS:
                nc.vector.quantize_mx(
                    out=xy_codes[:, first:end, :].rearrange("p g r -> p (g r)").bitcast(FP8X4),
                    scales=xy_scales[:, first:end, :].rearrange("p g r -> p (g r)"),
                    in_=grouped[t][:, first:end].rearrange("p g r t -> p (g r t)"),
                )
            codes[t] = (xy_codes, xy_scales)

        def multiply(t):
            xy_codes, xy_scales = codes[t]
            acc[t] = psum_y.tile([P, D], F32, name="acc")
            for g in range(PASSES):
                nc.tensor.matmul_mx(
                    out=acc[t][:],
                    lhsT=xy_codes[:, g, :].bitcast(FP8X4),
                    lhsT_scale=xy_scales[:, g, :],
                    rhs=dec_codes[:, g, :].bitcast(FP8X4),
                    rhs_scale=dec_scales[:, g, :],
                    start=(g == 0),
                    stop=(g == PASSES - 1),
                )

        def new_stat(name, t, width):
            stat[(name, t)] = small.tile([P, width], F32, name=name)
            return stat[(name, t)]

        def first_stats(t):
            nc.vector.bn_stats(out=new_stat("partial", t, 6)[:], in_=acc[t][:])

        def first_mean_var(t):
            nc.vector.bn_aggr(out=new_stat("mean_var", t, 2)[:], in_=stat[("partial", t)][:])

        def first_rstd(t):
            nc.scalar.activation(
                out=new_stat("rstd1", t, 1)[:],
                in_=stat[("mean_var", t)][:, 1:2],
                func=ACT.Abs_reciprocal_sqrt,
                bias=eps_ln[:],
            )

        def centre_and_gain(t):
            centred[t] = work.tile([P, D], F32, name="centred")
            nc.vector.scalar_tensor_tensor(
                out=centred[t][:],
                in0=acc[t][:],
                scalar=stat[("mean_var", t)][:, 0:1],
                in1=gain[:],
                op0=ALU.subtract,
                op1=ALU.mult,
            )

        def add_residual(t):
            z[t] = work.tile([P, D], F32, name="z")
            nc.vector.scalar_tensor_tensor(
                out=z[t][:],
                in0=centred[t][:],
                scalar=stat[("rstd1", t)][:],
                in1=x_tiles[t // PAIR][:, t % PAIR, :],
                op0=ALU.mult,
                op1=ALU.add,
                accum_out=new_stat("z_sum", t, 1)[:],
            )
            nc.gpsimd.tensor_scalar(
                out=new_stat("neg_mean", t, 1)[:],
                in0=stat[("z_sum", t)][:],
                scalar1=-1.0 / float(D),
                scalar2=0.0,
                op0=ALU.mult,
                op1=ALU.add,
            )

        def second_sum_of_squares(t):
            squares = work.tile([P, D], F32, name="squares")
            nc.scalar.activation(
                out=squares[:],
                in_=z[t][:],
                func=ACT.Square,
                scale=-float(D),
                bias=stat[("z_sum", t)][:],
                accum_out=new_stat("sum_sq", t, 1)[:],
            )

        def second_rstd(t):
            nc.scalar.activation(
                out=new_stat("rstd2", t, 1)[:],
                in_=stat[("sum_sq", t)][:],
                func=ACT.Abs_reciprocal_sqrt,
                scale=1.0 / float(D * D * D),
                bias=eps_ln[:],
            )

        def second_shift(t):
            nc.scalar.activation(
                out=new_stat("shift2", t, 1)[:],
                in_=stat[("neg_mean", t)][:],
                func=ACT.Identity,
                scale=stat[("rstd2", t)][:],
            )

        def normalise_on_scalar(t):
            result = work.tile([P, D], F32, name="result")
            nc.scalar.activation(
                out=result[:],
                in_=z[t][:],
                func=ACT.Identity,
                scale=stat[("rstd2", t)][:],
                bias=stat[("shift2", t)][:],
            )
            nc.sync.dma_start(out=out_view[:, t, :], in_=result[:])

        def normalise_on_vector(t):
            result = work.tile([P, D], F32, name="result")
            nc.vector.tensor_scalar(
                out=result[:],
                in0=z[t][:],
                scalar1=stat[("neg_mean", t)][:],
                scalar2=stat[("rstd2", t)][:],
                op0=ALU.add,
                op1=ALU.mult,
            )
            nc.sync.dma_start(out=out_view[:, t, :], in_=result[:])

        def live(t):
            return 0 <= t < TILES

        LAST = TILES - 1
        for t in range(-4, TILES + 2):
            if live(t):
                first_stats(t)
            if live(t + 2):
                quantise_tile(t + 2)
                multiply(t + 2)
            if live(t + 4):
                transpose_tile(t + 4)
            if live(t):
                first_mean_var(t)
            if live(t - 2):
                second_rstd(t - 2)
            if live(t + 3):
                evacuate_tile(t + 3)
            if live(t - 2) and t - 2 != LAST:
                second_shift(t - 2)
            if live(t):
                first_rstd(t)
            if live(t - 2) and t - 2 != LAST:
                normalise_on_scalar(t - 2)
            if t - 2 == LAST:
                normalise_on_vector(LAST)
            if live(t - 1):
                add_residual(t - 1)
                second_sum_of_squares(t - 1)
            if live(t):
                centre_and_gain(t)
